import numpy as np
import ml_dtypes


def mxq(x, axis, fmt="e4m3"):
    dtype, down = {"e4m3": (ml_dtypes.float8_e4m3fn, 7), "e5m2": (ml_dtypes.float8_e5m2, 14)}[fmt]
    v = np.moveaxis(np.asarray(x, np.float32).astype(ml_dtypes.bfloat16).astype(np.float64), axis, -1)
    blocks = v.reshape(v.shape[:-1] + (-1, 32))
    amax = np.abs(blocks).max(-1, keepdims=True)
    byte = np.maximum(np.where(amax > 0, np.frexp(amax)[1] - 1 + 127, 0) - down, 1)
    scale = np.exp2(byte - 127.0)
    codes = (blocks / scale).astype(np.float32).astype(dtype).astype(np.float64)
    return np.moveaxis((codes * scale).reshape(v.shape), -1, axis)


WIDE = False


def mx_kscale(k):
    if not WIDE:
        return np.ones(k)
    levels = np.array([10, -10, 5, -5, 0])
    a = np.random.permutation(np.resize(levels, k // 512 * 4)).reshape(k // 512, 4)
    idx = np.arange(k)
    return np.exp2(a[idx // 512, idx % 128 // 32])


BF16 = ml_dtypes.bfloat16


def bf(x):
    return np.asarray(x, np.float32).astype(BF16)


def f64(x):
    return np.asarray(x).astype(np.float64)


C, G, P, E = 8192, 1024, 8, 64


def setup_inputs():
    s = mx_kscale(G)
    return {"x": bf(np.random.standard_normal((C, G)) * s),
            "mask": bf(np.random.randint(0, 2, (G, P))),
            "W": bf(np.random.standard_normal((G, P * E)) * 1.4 / np.sqrt(G) / s[:, None]),
            "b": bf(np.random.standard_normal(P * E) * 0.3)}


def reference(x, mask, W, b):
    mask_rep = np.repeat(f64(mask), E, axis=1)
    out = (mxq(f64(x), 1, "e4m3") @ mxq(f64(W) * mask_rep, 0, "e4m3")) + f64(b)
    out = out.reshape(C, E, P).transpose(0, 2, 1)
    return out

@@ -1,0 +1,180 @@
+from contextlib import ExitStack
+
+import concourse.mybir as mybir
+from concourse.masks import make_identity
+
+F32 = mybir.dt.float32
+BF16 = mybir.dt.bfloat16
+U32 = mybir.dt.uint32
+U8 = mybir.dt.uint8
+FP8X4 = mybir.dt.float8_e4m3fn_x4
+ADD = mybir.AluOpType.add
+MULT = mybir.AluOpType.mult
+
+C, G, NP, E = 8192, 1024, 8, 64
+J = NP * E
+P = 128
+NT = C // P
+GT = 4
+NG = NT // GT
+FLOPS = 2 * C * G * J
+
+LL = 7
+XB = 8
+OB = 5
+LA = 1
+GB = 3
+CB = 3
+
+
+def tile_featureembed_t_kernel(tc, x, mask, W, b, out):
+    nc = tc.nc
+    x_view = x.rearrange("(p t) k -> p t k", t=NT)
+    out_view = out.rearrange("(p t) a e -> p t (a e)", t=NT)
+
+    with ExitStack() as ctx:
+        const = ctx.enter_context(tc.tile_pool(name="const", bufs=1))
+        xpool = ctx.enter_context(tc.tile_pool(name="xpool", bufs=XB))
+        gpool = ctx.enter_context(tc.tile_pool(name="gpool", bufs=GB))
+        cpool = ctx.enter_context(tc.tile_pool(name="cpool", bufs=CB))
+        opool = ctx.enter_context(tc.tile_pool(name="opool", bufs=OB))
+        psum = ctx.enter_context(tc.psum_pool(name="psum", bufs=1))
+        ctx.enter_context(tc.manual_schedule())
+
+        brow = const.tile([P, J], BF16, name="brow")
+        ones = const.tile([P, P], BF16, name="ones")
+        ident = const.tile([P, P], F32, name="ident")
+        nc.gpsimd.memset(brow[:], 0.0)
+        nc.gpsimd.memset(ones[:], 1.0)
+        make_identity(nc, ident[:])
+
+        mk = const.tile([P, 64], BF16, name="mk")
+        nc.scalar.dma_start(
+            out=mk[:].rearrange("q (a r) -> q a r", a=4),
+            in_=mask.rearrange("(a q e) m -> q a (e m)", a=4, q=P, e=2),
+        )
+        nc.scalar.dma_start(out=brow[0:1, :], in_=b.unsqueeze(0))
+
+        w_raw = const.tile([P, 4096], BF16, name="w_raw")
+        for g in range(2):
+            nc.sync.dma_start(
+                out=w_raw[:, g * 2048 : (g + 1) * 2048].rearrange("q (u r) -> q u r", u=2),
+                in_=W[g * 512 : (g + 1) * 512, :].rearrange("(u q e) j -> q u (e j)", u=2, q=P, e=2),
+            )
+
+        x_tiles = {}
+
+        def load(s):
+            x_sb = xpool.tile([P, GT, G], BF16, name="x_sb", tag="x_sb")
+            nc.sync.dma_start(out=x_sb[:], in_=x_view[:, s * GT : (s + 1) * GT, :])
+            x_tiles[s] = x_sb
+
+        for s in range(LL):
+            load(s)
+
+        mk_exp = const.tile([P, 512], BF16, name="mk_exp")
+        nc.vector.tensor_copy(
+            out=mk_exp[:].rearrange("q (r i) -> q r i", i=8),
+            in_=mk[:].unsqueeze(2).to_broadcast([P, 64, 8]),
+        )
+        w_grp = const.tile([P, 4096], BF16, name="w_grp", align_bytes=64)
+        w_codes = const.tile([P, 1024], U32, name="w_codes", align_bytes=64)
+        w_scales = const.tile([P, 1024], U8, name="w_scales", align_bytes=64)
+        for g in range(2):
+            nc.vector.tensor_tensor(
+                out=w_grp[:, g * 2048 : (g + 1) * 2048].rearrange("q (a e t) -> q a e t", a=NP, t=4),
+                in0=w_raw[:, g * 2048 : (g + 1) * 2048].rearrange("q (t e a) -> q a e t", t=4, a=NP),
+                in1=mk_exp[:, g * 256 : (g + 1) * 256]
+                .rearrange("q (t e) -> q e t", t=4)
+                .unsqueeze(1)
+                .to_broadcast([P, NP, E, 4]),
+                op=MULT,
+            )
+        for g in range(2):
+            nc.vector.quantize_mx(
+                out=w_codes[:, g * 512 : (g + 1) * 512].bitcast(FP8X4),
+                scales=w_scales[:, g * 512 : (g + 1) * 512],
+                in_=w_grp[:, g * 2048 : (g + 1) * 2048],
+            )
+
+        grp_tiles = {}
+        code_tiles = {}
+
+        def transposes(s):
+            x_f = x_tiles[s][:].bitcast(F32)
+            grp = gpool.tile([P, GT * 1024], BF16, name="grp", tag="grp", align_bytes=64)
+            grp_f = grp[:].bitcast(F32)
+            grp_tiles[s] = grp
+            banks = []
+            for i in range(GT):
+                xt = psum.tile([P, 4, P], F32, name="xt%d" % i, tag="xt%d" % i)
+                for a in range(4):
+                    nc.tensor.transpose(xt[:, a, :], x_f[:, i, a * P : (a + 1) * P], ident[:])
+                banks.append(xt)
+            for i in range(GT):
+                nc.scalar.copy(
+                    out=grp_f[:, i * 512 : (i + 1) * 512].rearrange("q (g c u) -> q g c u", g=2, u=2),
+                    in_=banks[i][:].rearrange("q (g u) c -> q g c u", u=2),
+                )
+
+        def quantise(s, h):
+            if h == 0:
+                codes = cpool.tile([P, GT * 256], U32, name="codes", tag="codes", align_bytes=64)
+                scales = cpool.tile([P, GT * 256], U8, name="scales", tag="scales", align_bytes=64)
+                code_tiles[s] = (codes, scales)
+            codes, scales = code_tiles[s]
+            nc.vector.quantize_mx(
+                out=codes[:, h * 512 : (h + 1) * 512].bitcast(FP8X4),
+                scales=scales[:, h * 512 : (h + 1) * 512],
+                in_=grp_tiles[s][:, h * 2048 : (h + 1) * 2048],
+            )
+
+        def multiply(s):
+            codes, scales = code_tiles[s]
+            banks = []
+            for i in range(GT):
+                y = psum.tile([P, J], F32, name="y%d" % i, tag="y%d" % i)
+                for g in range(2):
+                    cols = slice((i * 2 + g) * P, (i * 2 + g + 1) * P)
+                    nc.tensor.matmul_mx(
+                        out=y[:],
+                        lhsT=codes[:, cols].bitcast(FP8X4),
+                        lhsT_scale=scales[:, cols],
+                        rhs=w_codes[:, g * 512 : (g + 1) * 512].bitcast(FP8X4),
+                        rhs_scale=w_scales[:, g * 512 : (g + 1) * 512],
+                        start=(g == 0),
+                        stop=(g == 1),
+                    )
+                banks.append(y)
+            return banks
+
+        bias = const.tile([P, J], F32, name="bias")
+
+        def make_bias():
+            yb = psum.tile([P, J], F32, name="yb", tag="y0")
+            nc.tensor.matmul(out=yb[:], lhsT=ones[:], rhs=brow[:], start=True, stop=True)
+            nc.scalar.copy(
+                out=bias[:].rearrange("q (a e) -> q a e", a=NP),
+                in_=yb[:].rearrange("q (e a) -> q a e", a=NP),
+            )
+
+        for s in range(NG + LA):
+            if s + LL < NG:
+                load(s + LL)
+            if s < NG:
+                transposes(s)
+            if s == 0:
+                make_bias()
+            m = s - LA
+            banks = multiply(m) if m >= 0 else None
+            o_sb = None
+            if m >= 0:
+                o_sb = opool.tile([P, GT, J], F32, name="o_sb", tag="o_sb")
+            for h in range(2):
+                if s < NG:
+                    quantise(s, h)
+                if m >= 0:
+                    for i in (2 * h, 2 * h + 1):
+                        nc.vector.tensor_tensor(out=o_sb[:, i, :], in0=banks[i][:], in1=bias[:], op=ADD)
+            if m >= 0:
+                nc.sync.dma_start(out=out_view[:, m * GT : (m + 1) * GT, :], in_=o_sb[:])

@@ -15,16 +15,19 @@ C, G, NP, E = 8192, 1024, 8, 64
 J = NP * E
 P = 128
 NT = C // P
-GT = 4
-NG = NT // GT
 FLOPS = 2 * C * G * J
 
-LL = 7
-XB = 8
-OB = 5
+RUNS = [4,4,4,4,4,4,4,4,4,4,4,4,4,4,4,2,2]
+LOADS = [4,4,4,4,8,8,8,8,8,8]
+STORES = [4,4,4,4,4,4,4,4,4,4,4,4,4,4,4,2,2]
+XBUFS = {4:4,8:3}
+OBUFS = {2:2,4:6}
+LEAD = 24
+QW = 2
+GBQ = 6
+CBQ = 6
 LA = 1
-GB = 3
-CB = 3
+assert sum(RUNS) == NT and sum(LOADS) == NT and sum(STORES) == NT
 
 
 def tile_featureembed_t_kernel(tc, x, mask, W, b, out):
@@ -34,10 +37,10 @@ def tile_featureembed_t_kernel(tc, x, mask, W, b, out):
 
     with ExitStack() as ctx:
         const = ctx.enter_context(tc.tile_pool(name="const", bufs=1))
-        xpool = ctx.enter_context(tc.tile_pool(name="xpool", bufs=XB))
-        gpool = ctx.enter_context(tc.tile_pool(name="gpool", bufs=GB))
-        cpool = ctx.enter_context(tc.tile_pool(name="cpool", bufs=CB))
-        opool = ctx.enter_context(tc.tile_pool(name="opool", bufs=OB))
+        xpool = ctx.enter_context(tc.tile_pool(name="xpool", bufs=1))
+        gpool = ctx.enter_context(tc.tile_pool(name="gpool", bufs=GBQ))
+        cpool = ctx.enter_context(tc.tile_pool(name="cpool", bufs=CBQ))
+        opool = ctx.enter_context(tc.tile_pool(name="opool", bufs=1))
         psum = ctx.enter_context(tc.psum_pool(name="psum", bufs=1))
         ctx.enter_context(tc.manual_schedule())
 
@@ -62,15 +65,29 @@ def tile_featureembed_t_kernel(tc, x, mask, W, b, out):
                 in_=W[g * 512 : (g + 1) * 512, :].rearrange("(u q e) j -> q u (e j)", u=2, q=P, e=2),
             )
 
-        x_tiles = {}
+        x_of = {}
+        load_first = []
+        t0 = 0
+        for n in LOADS:
+            load_first.append(t0)
+            t0 += n
+        state = {"next_load": 0}
 
-        def load(s):
-            x_sb = xpool.tile([P, GT, G], BF16, name="x_sb", tag="x_sb")
-            nc.sync.dma_start(out=x_sb[:], in_=x_view[:, s * GT : (s + 1) * GT, :])
-            x_tiles[s] = x_sb
+        def issue_loads(limit):
+            while state["next_load"] < len(LOADS):
+                li = state["next_load"]
+                n = LOADS[li]
+                first = load_first[li]
+                if first + n > limit:
+                    break
+                x_sb = xpool.tile([P, n, G], BF16, name="x%d" % n, tag="x%d" % n, bufs=XBUFS[n])
+                nc.sync.dma_start(out=x_sb[:], in_=x_view[:, first : first + n, :])
+                x_f = x_sb[:].bitcast(F32)
+                for k in range(n):
+                    x_of[first + k] = (x_f, k)
+                state["next_load"] = li + 1
 
-        for s in range(LL):
-            load(s)
+        issue_loads(LEAD)
 
         mk_exp = const.tile([P, 512], BF16, name="mk_exp")
         nc.vector.tensor_copy(
@@ -97,57 +114,6 @@ def tile_featureembed_t_kernel(tc, x, mask, W, b, out):
                 in_=w_grp[:, g * 2048 : (g + 1) * 2048],
             )
 
-        grp_tiles = {}
-        code_tiles = {}
-
-        def transposes(s):
-            x_f = x_tiles[s][:].bitcast(F32)
-            grp = gpool.tile([P, GT * 1024], BF16, name="grp", tag="grp", align_bytes=64)
-            grp_f = grp[:].bitcast(F32)
-            grp_tiles[s] = grp
-            banks = []
-            for i in range(GT):
-                xt = psum.tile([P, 4, P], F32, name="xt%d" % i, tag="xt%d" % i)
-                for a in range(4):
-                    nc.tensor.transpose(xt[:, a, :], x_f[:, i, a * P : (a + 1) * P], ident[:])
-                banks.append(xt)
-            for i in range(GT):
-                nc.scalar.copy(
-                    out=grp_f[:, i * 512 : (i + 1) * 512].rearrange("q (g c u) -> q g c u", g=2, u=2),
-                    in_=banks[i][:].rearrange("q (g u) c -> q g c u", u=2),
-                )
-
-        def quantise(s, h):
-            if h == 0:
-                codes = cpool.tile([P, GT * 256], U32, name="codes", tag="codes", align_bytes=64)
-                scales = cpool.tile([P, GT * 256], U8, name="scales", tag="scales", align_bytes=64)
-                code_tiles[s] = (codes, scales)
-            codes, scales = code_tiles[s]
-            nc.vector.quantize_mx(
-                out=codes[:, h * 512 : (h + 1) * 512].bitcast(FP8X4),
-                scales=scales[:, h * 512 : (h + 1) * 512],
-                in_=grp_tiles[s][:, h * 2048 : (h + 1) * 2048],
-            )
-
-        def multiply(s):
-            codes, scales = code_tiles[s]
-            banks = []
-            for i in range(GT):
-                y = psum.tile([P, J], F32, name="y%d" % i, tag="y%d" % i)
-                for g in range(2):
-                    cols = slice((i * 2 + g) * P, (i * 2 + g + 1) * P)
-                    nc.tensor.matmul_mx(
-                        out=y[:],
-                        lhsT=codes[:, cols].bitcast(FP8X4),
-                        lhsT_scale=scales[:, cols],
-                        rhs=w_codes[:, g * 512 : (g + 1) * 512].bitcast(FP8X4),
-                        rhs_scale=w_scales[:, g * 512 : (g + 1) * 512],
-                        start=(g == 0),
-                        stop=(g == 1),
-                    )
-                banks.append(y)
-            return banks
-
         bias = const.tile([P, J], F32, name="bias")
 
         def make_bias():
@@ -158,23 +124,107 @@ def tile_featureembed_t_kernel(tc, x, mask, W, b, out):
                 in_=yb[:].rearrange("q (e a) -> q a e", a=NP),
             )
 
-        for s in range(NG + LA):
-            if s + LL < NG:
-                load(s + LL)
-            if s < NG:
-                transposes(s)
+        run_first = []
+        t0 = 0
+        for n in RUNS:
+            run_first.append(t0)
+            t0 += n
+        chunks = []
+        chunk_of = {}
+        run_chunks = []
+        for r in range(len(RUNS)):
+            mine = []
+            for o in range(0, RUNS[r], QW):
+                w = min(QW, RUNS[r] - o)
+                mine.append(len(chunks))
+                for k in range(w):
+                    chunk_of[run_first[r] + o + k] = (len(chunks), k)
+                chunks.append((run_first[r] + o, w))
+            run_chunks.append(mine)
+        store_of = {}
+        t0 = 0
+        for si in range(len(STORES)):
+            for k in range(STORES[si]):
+                store_of[t0 + k] = (si, k, t0)
+            t0 += STORES[si]
+
+        grp_of = {}
+        code_of = {}
+        o_of = {}
+        y_of = {}
+
+        def transpose_tile(t):
+            q, k = chunk_of[t]
+            w = chunks[q][1]
+            if k == 0:
+                grp_of[q] = gpool.tile([P, QW * 1024], BF16, name="grp", tag="grp", align_bytes=64)
+            grp_f = grp_of[q][:].bitcast(F32)
+            x_f, i = x_of[t]
+            xt = psum.tile([P, 4, P], F32, name="xt%d" % (t % 4), tag="xt%d" % (t % 4))
+            for a in range(4):
+                nc.tensor.transpose(xt[:, a, :], x_f[:, i, a * P : (a + 1) * P], ident[:])
+            nc.scalar.copy(
+                out=grp_f[:, k * 512 : (k + 1) * 512].rearrange("q (g c u) -> q g c u", g=2, u=2),
+                in_=xt[:].rearrange("q (g u) c -> q g c u", u=2),
+            )
+
+        def quantise(q):
+            w = chunks[q][1]
+            codes = cpool.tile([P, QW * 256], U32, name="codes", tag="codes", align_bytes=64)
+            scales = cpool.tile([P, QW * 256], U8, name="scales", tag="scales", align_bytes=64)
+            code_of[q] = (codes, scales)
+            nc.vector.quantize_mx(
+                out=codes[:, 0 : w * 256].bitcast(FP8X4),
+                scales=scales[:, 0 : w * 256],
+                in_=grp_of[q][:, 0 : w * 1024],
+            )
+
+        def multiply(t):
+            q, k = chunk_of[t]
+            codes, scales = code_of[q]
+            y = psum.tile([P, J], F32, name="y%d" % (t % 4), tag="y%d" % (t % 4))
+            for g in range(2):
+                cols = slice((k * 2 + g) * P, (k * 2 + g + 1) * P)
+                nc.tensor.matmul_mx(
+                    out=y[:],
+                    lhsT=codes[:, cols].bitcast(FP8X4),
+                    lhsT_scale=scales[:, cols],
+                    rhs=w_codes[:, g * 512 : (g + 1) * 512].bitcast(FP8X4),
+                    rhs_scale=w_scales[:, g * 512 : (g + 1) * 512],
+                    start=(g == 0),
+                    stop=(g == 1),
+                )
+            y_of[t] = y
+
+        def add_bias(t):
+            si, k, first = store_of[t]
+            n = STORES[si]
+            if k == 0:
+                o_of[si] = opool.tile([P, n, J], F32, name="o%d" % n, tag="o%d" % n, bufs=OBUFS[n])
+            o_sb = o_of[si]
+            nc.vector.tensor_tensor(out=o_sb[:, k, :], in0=y_of[t][:], in1=bias[:], op=ADD)
+            if k == n - 1:
+                nc.sync.dma_start(out=out_view[:, first : first + n, :], in_=o_sb[:])
+
+        NR = len(RUNS)
+        for s in range(NR + LA):
+            if s < NR:
+                for t in range(run_first[s], run_first[s] + RUNS[s]):
+                    transpose_tile(t)
+                issue_loads(run_first[s] + RUNS[s] + LEAD)
             if s == 0:
                 make_bias()
             m = s - LA
-            banks = multiply(m) if m >= 0 else None
-            o_sb = None
-            if m >= 0:
-                o_sb = opool.tile([P, GT, J], F32, name="o_sb", tag="o_sb")
-            for h in range(2):
-                if s < NG:
-                    quantise(s, h)
-                if m >= 0:
-                    for i in (2 * h, 2 * h + 1):
-                        nc.vector.tensor_tensor(out=o_sb[:, i, :], in0=banks[i][:], in1=bias[:], op=ADD)
-            if m >= 0:
-                nc.sync.dma_start(out=out_view[:, m * GT : (m + 1) * GT, :], in_=o_sb[:])
+            qs = run_chunks[s] if s < NR else []
+            ts = list(range(run_first[m], run_first[m] + RUNS[m])) if m >= 0 else []
+            per = (len(ts) + len(qs) - 1) // len(qs) if qs else len(ts)
+            done = 0
+            for q in qs:
+                quantise(q)
+                for t in ts[done : done + per]:
+                    multiply(t)
+                    add_bias(t)
+                done += per
+            for t in ts[done:]:
+                multiply(t)
+                add_bias(t)

@@ -98,15 +98,20 @@ def tile_featureembed_t_kernel(tc, x, mask, W, b, out):
         w_codes = const.tile([P, 1024], U32, name="w_codes", align_bytes=64)
         w_scales = const.tile([P, 1024], U8, name="w_scales", align_bytes=64)
         for g in range(2):
-            nc.vector.tensor_tensor(
-                out=w_grp[:, g * 2048 : (g + 1) * 2048].rearrange("q (a e t) -> q a e t", a=NP, t=4),
-                in0=w_raw[:, g * 2048 : (g + 1) * 2048].rearrange("q (t e a) -> q a e t", t=4, a=NP),
-                in1=mk_exp[:, g * 256 : (g + 1) * 256]
-                .rearrange("q (t e) -> q e t", t=4)
-                .unsqueeze(1)
-                .to_broadcast([P, NP, E, 4]),
-                op=MULT,
-            )
+            for h in range(2):
+                nc.vector.tensor_tensor(
+                    out=w_grp[:, g * 2048 + h * 1024 : g * 2048 + (h + 1) * 1024].rearrange(
+                        "q (a e t) -> q e t a", a=4, t=4
+                    ),
+                    in0=w_raw[:, g * 2048 : (g + 1) * 2048].rearrange("q (t e a) -> q e t a", t=4, a=NP)[
+                        :, :, :, h * 4 : (h + 1) * 4
+                    ],
+                    in1=mk_exp[:, g * 256 : (g + 1) * 256]
+                    .rearrange("q (t e) -> q e t", t=4)
+                    .unsqueeze(3)
+                    .to_broadcast([P, E, 4, 4]),
+                    op=MULT,
+                )
         for g in range(2):
             nc.vector.quantize_mx(
                 out=w_codes[:, g * 512 : (g + 1) * 512].bitcast(FP8X4),

@@ -17,10 +17,10 @@ P = 128
 NT = C // P
 FLOPS = 2 * C * G * J
 
-RUNS = [4,4,4,4,4,4,4,4,4,4,4,4,4,4,4,2,2]
-LOADS = [4,4,4,4,8,8,8,8,8,8]
+RUNS = [2,2,4,4,4,4,4,4,4,4,4,4,4,4,4,4,2,2]
+LOADS = [2,2,4,4,4,8,8,8,8,8,8]
 STORES = [4,4,4,4,4,4,4,4,4,4,4,4,4,4,4,2,2]
-XBUFS = {4:4,8:3}
+XBUFS = {2:2,4:3,8:3}
 OBUFS = {2:2,4:6}
 LEAD = 24
 QW = 2
@@ -89,35 +89,54 @@ def tile_featureembed_t_kernel(tc, x, mask, W, b, out):
 
         issue_loads(LEAD)
 
-        mk_exp = const.tile([P, 512], BF16, name="mk_exp")
-        nc.vector.tensor_copy(
-            out=mk_exp[:].rearrange("q (r i) -> q r i", i=8),
-            in_=mk[:].unsqueeze(2).to_broadcast([P, 64, 8]),
-        )
+        mk_grp = const.tile([P, 512], BF16, name="mk_grp")
+        for g in range(2):
+            nc.vector.tensor_copy(
+                out=mk_grp[:, g * 256 : (g + 1) * 256].rearrange("q (m i t) -> q m i t", m=8, t=4),
+                in_=mk[:, g * 32 : (g + 1) * 32]
+                .rearrange("q (t m) -> q m t", t=4)
+                .unsqueeze(2)
+                .to_broadcast([P, 8, 8, 4]),
+            )
         w_grp = const.tile([P, 4096], BF16, name="w_grp", align_bytes=64)
         w_codes = const.tile([P, 1024], U32, name="w_codes", align_bytes=64)
         w_scales = const.tile([P, 1024], U8, name="w_scales", align_bytes=64)
-        for g in range(2):
-            for h in range(2):
-                nc.vector.tensor_tensor(
-                    out=w_grp[:, g * 2048 + h * 1024 : g * 2048 + (h + 1) * 1024].rearrange(
-                        "q (a e t) -> q e t a", a=4, t=4
-                    ),
-                    in0=w_raw[:, g * 2048 : (g + 1) * 2048].rearrange("q (t e a) -> q e t a", t=4, a=NP)[
-                        :, :, :, h * 4 : (h + 1) * 4
-                    ],
-                    in1=mk_exp[:, g * 256 : (g + 1) * 256]
-                    .rearrange("q (t e) -> q e t", t=4)
-                    .unsqueeze(3)
-                    .to_broadcast([P, E, 4, 4]),
-                    op=MULT,
-                )
-        for g in range(2):
+        def w_regroup(g, h):
+            dst = w_grp[:, g * 2048 + h * 1024 : g * 2048 + (h + 1) * 1024].rearrange(
+                "q (a e t) -> q e t a", a=4, t=4
+            )
+            src = w_raw[:, g * 2048 : (g + 1) * 2048].rearrange("q (t e a) -> q e t a", t=4, a=NP)[
+                :, :, :, h * 4 : (h + 1) * 4
+            ]
+            if h == 0:
+                nc.vector.tensor_copy(out=dst, in_=src)
+            else:
+                nc.scalar.copy(out=dst, in_=src)
+
+        def w_mask(g):
+            w_g = w_grp[:, g * 2048 : (g + 1) * 2048].rearrange("q (a r) -> q a r", a=NP)
+            nc.vector.tensor_tensor(
+                out=w_g,
+                in0=w_g,
+                in1=mk_grp[:, g * 256 : (g + 1) * 256].unsqueeze(1).to_broadcast([P, NP, 256]),
+                op=MULT,
+            )
+
+        def w_quantise(g):
             nc.vector.quantize_mx(
                 out=w_codes[:, g * 512 : (g + 1) * 512].bitcast(FP8X4),
                 scales=w_scales[:, g * 512 : (g + 1) * 512],
                 in_=w_grp[:, g * 2048 : (g + 1) * 2048],
             )
+
+        w_regroup(0, 0)
+        w_regroup(0, 1)
+        w_regroup(1, 1)
+        w_mask(0)
+        w_regroup(1, 0)
+        w_quantise(0)
+        w_mask(1)
+        w_quantise(1)
 
         bias = const.tile([P, J], F32, name="bias")
 

@@ -17,10 +17,10 @@ P = 128
 NT = C // P
 FLOPS = 2 * C * G * J
 
-RUNS = [2,2,4,4,4,4,4,4,4,4,4,4,4,4,4,4,2,2]
-LOADS = [2,2,4,4,4,8,8,8,8,8,8]
+RUNS = [4,4,4,4,4,4,4,4,4,4,4,4,4,4,4,2,2]
+LOADS = [4,4,4,4,8,8,8,8,8,8]
 STORES = [4,4,4,4,4,4,4,4,4,4,4,4,4,4,4,2,2]
-XBUFS = {2:2,4:3,8:3}
+XBUFS = {4:4,8:3}
 OBUFS = {2:2,4:6}
 LEAD = 24
 QW = 2
@@ -89,54 +89,35 @@ def tile_featureembed_t_kernel(tc, x, mask, W, b, out):
 
         issue_loads(LEAD)
 
-        mk_grp = const.tile([P, 512], BF16, name="mk_grp")
-        for g in range(2):
-            nc.vector.tensor_copy(
-                out=mk_grp[:, g * 256 : (g + 1) * 256].rearrange("q (m i t) -> q m i t", m=8, t=4),
-                in_=mk[:, g * 32 : (g + 1) * 32]
-                .rearrange("q (t m) -> q m t", t=4)
-                .unsqueeze(2)
-                .to_broadcast([P, 8, 8, 4]),
-            )
+        mk_exp = const.tile([P, 512], BF16, name="mk_exp")
+        nc.vector.tensor_copy(
+            out=mk_exp[:].rearrange("q (r i) -> q r i", i=8),
+            in_=mk[:].unsqueeze(2).to_broadcast([P, 64, 8]),
+        )
         w_grp = const.tile([P, 4096], BF16, name="w_grp", align_bytes=64)
         w_codes = const.tile([P, 1024], U32, name="w_codes", align_bytes=64)
         w_scales = const.tile([P, 1024], U8, name="w_scales", align_bytes=64)
-        def w_regroup(g, h):
-            dst = w_grp[:, g * 2048 + h * 1024 : g * 2048 + (h + 1) * 1024].rearrange(
-                "q (a e t) -> q e t a", a=4, t=4
-            )
-            src = w_raw[:, g * 2048 : (g + 1) * 2048].rearrange("q (t e a) -> q e t a", t=4, a=NP)[
-                :, :, :, h * 4 : (h + 1) * 4
-            ]
-            if h == 0:
-                nc.vector.tensor_copy(out=dst, in_=src)
-            else:
-                nc.scalar.copy(out=dst, in_=src)
-
-        def w_mask(g):
-            w_g = w_grp[:, g * 2048 : (g + 1) * 2048].rearrange("q (a r) -> q a r", a=NP)
-            nc.vector.tensor_tensor(
-                out=w_g,
-                in0=w_g,
-                in1=mk_grp[:, g * 256 : (g + 1) * 256].unsqueeze(1).to_broadcast([P, NP, 256]),
-                op=MULT,
-            )
-
-        def w_quantise(g):
+        for g in range(2):
+            for h in range(2):
+                nc.vector.tensor_tensor(
+                    out=w_grp[:, g * 2048 + h * 1024 : g * 2048 + (h + 1) * 1024].rearrange(
+                        "q (a e t) -> q e t a", a=4, t=4
+                    ),
+                    in0=w_raw[:, g * 2048 : (g + 1) * 2048].rearrange("q (t e a) -> q e t a", t=4, a=NP)[
+                        :, :, :, h * 4 : (h + 1) * 4
+                    ],
+                    in1=mk_exp[:, g * 256 : (g + 1) * 256]
+                    .rearrange("q (t e) -> q e t", t=4)
+                    .unsqueeze(3)
+                    .to_broadcast([P, E, 4, 4]),
+                    op=MULT,
+                )
+        for g in range(2):
             nc.vector.quantize_mx(
                 out=w_codes[:, g * 512 : (g + 1) * 512].bitcast(FP8X4),
                 scales=w_scales[:, g * 512 : (g + 1) * 512],
                 in_=w_grp[:, g * 2048 : (g + 1) * 2048],
             )
-
-        w_regroup(0, 0)
-        w_regroup(0, 1)
-        w_regroup(1, 1)
-        w_mask(0)
-        w_regroup(1, 0)
-        w_quantise(0)
-        w_mask(1)
-        w_quantise(1)
 
         bias = const.tile([P, J], F32, name="bias")
 
@@ -228,7 +209,8 @@ def tile_featureembed_t_kernel(tc, x, mask, W, b, out):
             o_sb = o_of[si]
             nc.vector.tensor_tensor(out=o_sb[:, k, :], in0=y_of[t][:], in1=bias[:], op=ADD)
             if k == n - 1:
-                nc.sync.dma_start(out=out_view[:, first : first + n, :], in_=o_sb[:])
+                queue = nc.gpsimd if first < 32 else nc.sync
+                queue.dma_start(out=out_view[:, first : first + n, :], in_=o_sb[:])
 
         NR = len(RUNS)
         for s in range(NR + LA):

from contextlib import ExitStack

import concourse.mybir as mybir
from concourse.masks import make_identity

F32 = mybir.dt.float32
BF16 = mybir.dt.bfloat16
U32 = mybir.dt.uint32
U8 = mybir.dt.uint8
FP8X4 = mybir.dt.float8_e4m3fn_x4
ADD = mybir.AluOpType.add
MULT = mybir.AluOpType.mult

C, G, NP, E = 8192, 1024, 8, 64
J = NP * E
P = 128
NT = C // P
FLOPS = 2 * C * G * J

RUNS = [4,4,4,4,4,4,4,4,4,4,4,4,4,4,4,2,2]
LOADS = [4,4,4,4,8,8,8,8,8,8]
STORES = [4,4,4,4,4,4,4,4,4,4,4,4,4,4,4,2,2]
XBUFS = {4:4,8:3}
OBUFS = {2:2,4:6}
LEAD = 24
QW = 2
GBQ = 6
CBQ = 6
LA = 1
assert sum(RUNS) == NT and sum(LOADS) == NT and sum(STORES) == NT


def tile_featureembed_t_kernel(tc, x, mask, W, b, out):
    nc = tc.nc
    x_view = x.rearrange("(p t) k -> p t k", t=NT)
    out_view = out.rearrange("(p t) a e -> p t (a e)", t=NT)

    with ExitStack() as ctx:
        const = ctx.enter_context(tc.tile_pool(name="const", bufs=1))
        xpool = ctx.enter_context(tc.tile_pool(name="xpool", bufs=1))
        gpool = ctx.enter_context(tc.tile_pool(name="gpool", bufs=GBQ))
        cpool = ctx.enter_context(tc.tile_pool(name="cpool", bufs=CBQ))
        opool = ctx.enter_context(tc.tile_pool(name="opool", bufs=1))
        psum = ctx.enter_context(tc.psum_pool(name="psum", bufs=1))
        ctx.enter_context(tc.manual_schedule())

        brow = const.tile([P, J], BF16, name="brow")
        ones = const.tile([P, P], BF16, name="ones")
        ident = const.tile([P, P], F32, name="ident")
        nc.gpsimd.memset(brow[:], 0.0)
        nc.gpsimd.memset(ones[:], 1.0)
        make_identity(nc, ident[:])

        mk = const.tile([P, 64], BF16, name="mk")
        nc.scalar.dma_start(
            out=mk[:].rearrange("q (a r) -> q a r", a=4),
            in_=mask.rearrange("(a q e) m -> q a (e m)", a=4, q=P, e=2),
        )
        nc.scalar.dma_start(out=brow[0:1, :], in_=b.unsqueeze(0))

        w_raw = const.tile([P, 4096], BF16, name="w_raw")
        for g in range(2):
            nc.sync.dma_start(
                out=w_raw[:, g * 2048 : (g + 1) * 2048].rearrange("q (u r) -> q u r", u=2),
                in_=W[g * 512 : (g + 1) * 512, :].rearrange("(u q e) j -> q u (e j)", u=2, q=P, e=2),
            )

        x_of = {}
        load_first = []
        t0 = 0
        for n in LOADS:
            load_first.append(t0)
            t0 += n
        state = {"next_load": 0}

        def issue_loads(limit):
            while state["next_load"] < len(LOADS):
                li = state["next_load"]
                n = LOADS[li]
                first = load_first[li]
                if first + n > limit:
                    break
                x_sb = xpool.tile([P, n, G], BF16, name="x%d" % n, tag="x%d" % n, bufs=XBUFS[n])
                nc.sync.dma_start(out=x_sb[:], in_=x_view[:, first : first + n, :])
                x_f = x_sb[:].bitcast(F32)
                for k in range(n):
                    x_of[first + k] = (x_f, k)
                state["next_load"] = li + 1

        issue_loads(LEAD)

        mk_exp = const.tile([P, 512], BF16, name="mk_exp")
        nc.vector.tensor_copy(
            out=mk_exp[:].rearrange("q (r i) -> q r i", i=8),
            in_=mk[:].unsqueeze(2).to_broadcast([P, 64, 8]),
        )
        w_grp = const.tile([P, 4096], BF16, name="w_grp", align_bytes=64)
        w_codes = const.tile([P, 1024], U32, name="w_codes", align_bytes=64)
        w_scales = const.tile([P, 1024], U8, name="w_scales", align_bytes=64)
        for g in range(2):
            for h in range(2):
                nc.vector.tensor_tensor(
                    out=w_grp[:, g * 2048 + h * 1024 : g * 2048 + (h + 1) * 1024].rearrange(
                        "q (a e t) -> q e t a", a=4, t=4
                    ),
                    in0=w_raw[:, g * 2048 : (g + 1) * 2048].rearrange("q (t e a) -> q e t a", t=4, a=NP)[
                        :, :, :, h * 4 : (h + 1) * 4
                    ],
                    in1=mk_exp[:, g * 256 : (g + 1) * 256]
                    .rearrange("q (t e) -> q e t", t=4)
                    .unsqueeze(3)
                    .to_broadcast([P, E, 4, 4]),
                    op=MULT,
                )
        for g in range(2):
            nc.vector.quantize_mx(
                out=w_codes[:, g * 512 : (g + 1) * 512].bitcast(FP8X4),
                scales=w_scales[:, g * 512 : (g + 1) * 512],
                in_=w_grp[:, g * 2048 : (g + 1) * 2048],
            )

        bias = const.tile([P, J], F32, name="bias")

        def make_bias():
            yb = psum.tile([P, J], F32, name="yb", tag="y0")
            nc.tensor.matmul(out=yb[:], lhsT=ones[:], rhs=brow[:], start=True, stop=True)
            nc.scalar.copy(
                out=bias[:].rearrange("q (a e) -> q a e", a=NP),
                in_=yb[:].rearrange("q (e a) -> q a e", a=NP),
            )

        run_first = []
        t0 = 0
        for n in RUNS:
            run_first.append(t0)
            t0 += n
        chunks = []
        chunk_of = {}
        run_chunks = []
        for r in range(len(RUNS)):
            mine = []
            for o in range(0, RUNS[r], QW):
                w = min(QW, RUNS[r] - o)
                mine.append(len(chunks))
                for k in range(w):
                    chunk_of[run_first[r] + o + k] = (len(chunks), k)
                chunks.append((run_first[r] + o, w))
            run_chunks.append(mine)
        store_of = {}
        t0 = 0
        for si in range(len(STORES)):
            for k in range(STORES[si]):
                store_of[t0 + k] = (si, k, t0)
            t0 += STORES[si]

        grp_of = {}
        code_of = {}
        o_of = {}
        y_of = {}

        def transpose_tile(t):
            q, k = chunk_of[t]
            w = chunks[q][1]
            if k == 0:
                grp_of[q] = gpool.tile([P, QW * 1024], BF16, name="grp", tag="grp", align_bytes=64)
            grp_f = grp_of[q][:].bitcast(F32)
            x_f, i = x_of[t]
            xt = psum.tile([P, 4, P], F32, name="xt%d" % (t % 4), tag="xt%d" % (t % 4))
            for a in range(4):
                nc.tensor.transpose(xt[:, a, :], x_f[:, i, a * P : (a + 1) * P], ident[:])
            nc.scalar.copy(
                out=grp_f[:, k * 512 : (k + 1) * 512].rearrange("q (g c u) -> q g c u", g=2, u=2),
                in_=xt[:].rearrange("q (g u) c -> q g c u", u=2),
            )

        def quantise(q):
            w = chunks[q][1]
            codes = cpool.tile([P, QW * 256], U32, name="codes", tag="codes", align_bytes=64)
            scales = cpool.tile([P, QW * 256], U8, name="scales", tag="scales", align_bytes=64)
            code_of[q] = (codes, scales)
            nc.vector.quantize_mx(
                out=codes[:, 0 : w * 256].bitcast(FP8X4),
                scales=scales[:, 0 : w * 256],
                in_=grp_of[q][:, 0 : w * 1024],
            )

        def multiply(t):
            q, k = chunk_of[t]
            codes, scales = code_of[q]
            y = psum.tile([P, J], F32, name="y%d" % (t % 4), tag="y%d" % (t % 4))
            for g in range(2):
                cols = slice((k * 2 + g) * P, (k * 2 + g + 1) * P)
                nc.tensor.matmul_mx(
                    out=y[:],
                    lhsT=codes[:, cols].bitcast(FP8X4),
                    lhsT_scale=scales[:, cols],
                    rhs=w_codes[:, g * 512 : (g + 1) * 512].bitcast(FP8X4),
                    rhs_scale=w_scales[:, g * 512 : (g + 1) * 512],
                    start=(g == 0),
                    stop=(g == 1),
                )
            y_of[t] = y

        def add_bias(t):
            si, k, first = store_of[t]
            n = STORES[si]
            if k == 0:
                o_of[si] = opool.tile([P, n, J], F32, name="o%d" % n, tag="o%d" % n, bufs=OBUFS[n])
            o_sb = o_of[si]
            nc.vector.tensor_tensor(out=o_sb[:, k, :], in0=y_of[t][:], in1=bias[:], op=ADD)
            if k == n - 1:
                queue = nc.gpsimd if first < 32 else nc.sync
                queue.dma_start(out=out_view[:, first : first + n, :], in_=o_sb[:])

        NR = len(RUNS)
        for s in range(NR + LA):
            if s < NR:
                for t in range(run_first[s], run_first[s] + RUNS[s]):
                    transpose_tile(t)
                issue_loads(run_first[s] + RUNS[s] + LEAD)
            if s == 0:
                make_bias()
            m = s - LA
            qs = run_chunks[s] if s < NR else []
            ts = list(range(run_first[m], run_first[m] + RUNS[m])) if m >= 0 else []
            per = (len(ts) + len(qs) - 1) // len(qs) if qs else len(ts)
            done = 0
            for q in qs:
                quantise(q)
                for t in ts[done : done + per]:
                    multiply(t)
                    add_bias(t)
                done += per
            for t in ts[done:]:
                multiply(t)
                add_bias(t)
